import numpy as np
import ml_dtypes


def mxq(x, axis, fmt="e4m3"):
    dtype, down = {"e4m3": (ml_dtypes.float8_e4m3fn, 7), "e5m2": (ml_dtypes.float8_e5m2, 14)}[fmt]
    v = np.moveaxis(np.asarray(x, np.float32).astype(ml_dtypes.bfloat16).astype(np.float64), axis, -1)
    blocks = v.reshape(v.shape[:-1] + (-1, 32))
    amax = np.abs(blocks).max(-1, keepdims=True)
    byte = np.maximum(np.where(amax > 0, np.frexp(amax)[1] - 1 + 127, 0) - down, 1)
    scale = np.exp2(byte - 127.0)
    codes = (blocks / scale).astype(np.float32).astype(dtype).astype(np.float64)
    return np.moveaxis((codes * scale).reshape(v.shape), -1, axis)


WIDE = False


def mx_kscale(k):
    if not WIDE:
        return np.ones(k)
    levels = np.array([10, -10, 5, -5, 0])
    a = np.random.permutation(np.resize(levels, k // 512 * 4)).reshape(k // 512, 4)
    idx = np.arange(k)
    return np.exp2(a[idx // 512, idx % 128 // 32])


BF16 = ml_dtypes.bfloat16


def bf(x):
    return np.asarray(x, np.float32).astype(BF16)


def f64(x):
    return np.asarray(x).astype(np.float64)


B, L, E, H, C, EO = 1, 1024, 2048, 16, 512, 2048
HD = E // H
G = L // C
NH = B * H


def setup_inputs():
    t = mx_kscale(C)
    return {"q_chunks": bf(np.random.standard_normal((NH, G, C, HD)) / np.sqrt(HD)),
            "k_chunks": bf(np.random.standard_normal((NH, G, C, HD)) * 0.5 * t[:, None]),
            "v_chunks": bf(np.random.standard_normal((NH, G, C, HD)) * 6.0 / np.sqrt(C) / t[:, None])}


def reference(q_chunks, k_chunks, v_chunks):
    logits = f64(q_chunks) @ f64(k_chunks).transpose(0, 1, 3, 2)
    p = np.maximum(logits, 0.0)
    return mxq(p, 3, "e4m3") @ mxq(f64(v_chunks), 2, "e4m3")

@@ -1,0 +1,140 @@
+from contextlib import ExitStack
+
+import concourse.mybir as mybir
+from concourse.masks import make_identity
+
+BF16 = mybir.dt.bfloat16
+F32 = mybir.dt.float32
+U32 = mybir.dt.uint32
+U8 = mybir.dt.uint8
+FP8X4 = mybir.dt.float8_e4m3fn_x4
+RELU = mybir.ActivationFunctionType.Relu
+
+P = 128
+PACK = 4
+SLICES = 32
+CHUNK = 512
+HEAD = 128
+LOAD_SLICES = 2
+
+FLOPS = 2 * 2 * SLICES * CHUNK * CHUNK * HEAD
+
+
+def tile_normlocalattention_pa_kernel(tc, q_chunks, k_chunks, v_chunks, out):
+    nc = tc.nc
+    q_rows = q_chunks.rearrange("n g (i j) d -> i (n g) j d", j=PACK)
+    k_rows = k_chunks.rearrange("n g (i j) d -> i (n g) j d", j=PACK)
+    v_rows = v_chunks.rearrange("n g (i j) d -> i (n g) j d", j=PACK)
+    out_rows = out.rearrange("n g (i j) d -> i (n g) j d", j=PACK)
+
+    with ExitStack() as ctx:
+        ctx.enter_context(tc.manual_schedule())
+        const = ctx.enter_context(tc.tile_pool(name="const", bufs=1))
+        inputs = ctx.enter_context(tc.tile_pool(name="inputs", bufs=1))
+        work = ctx.enter_context(tc.tile_pool(name="work", bufs=2))
+        mx_operands = ctx.enter_context(tc.tile_pool(name="mx_operands", bufs=3))
+        results = ctx.enter_context(tc.tile_pool(name="results", bufs=SLICES))
+        transposed_banks = ctx.enter_context(tc.psum_pool(name="transposed_banks", bufs=2))
+        score_banks = ctx.enter_context(tc.psum_pool(name="score_banks", bufs=4))
+        out_banks = ctx.enter_context(tc.psum_pool(name="out_banks", bufs=2))
+
+        k_in, q_in, v_in = [], [], []
+        for g in range(SLICES // LOAD_SLICES):
+            slices = slice(g * LOAD_SLICES, (g + 1) * LOAD_SLICES)
+            for label, rows, tiles in (("k", k_rows, k_in), ("q", q_rows, q_in), ("v", v_rows, v_in)):
+                loaded = inputs.tile([P, LOAD_SLICES, PACK, HEAD], BF16, name="%s_in%d" % (label, g))
+                nc.sync.dma_start(out=loaded[:], in_=rows[:, slices])
+                tiles.append(loaded)
+
+        identity = const.tile([P, P], BF16)
+        make_identity(nc, identity[:])
+
+        kqT_bank, kqT, p_bf, p_words, p_scales = {}, {}, {}, {}, {}
+        v_bf, v_words, v_scales, out_bank, out_sb = {}, {}, {}, {}, {}
+
+        def transpose_k_and_q(s):
+            g, h = divmod(s, LOAD_SLICES)
+            kqT_bank[s] = transposed_banks.tile([P, 2 * PACK, P], BF16, name="kqT_bank")
+            for t in range(PACK):
+                nc.tensor.transpose(kqT_bank[s][:, t, :], k_in[g][:, h, t, :], identity[:])
+            for j in range(PACK):
+                nc.tensor.transpose(kqT_bank[s][:, PACK + j, :], q_in[g][:, h, j, :], identity[:])
+
+        def copy_kT_and_qT(s):
+            kqT[s] = work.tile([P, 2 * PACK, P], BF16, name="kqT")
+            nc.vector.tensor_copy(out=kqT[s][:], in_=kqT_bank[s][:])
+
+        def scores_and_relu(s, j):
+            scores = score_banks.tile([P, PACK, P], F32, name="scores")
+            for t in range(PACK):
+                nc.tensor.matmul(
+                    scores[:, t, :], lhsT=kqT[s][:, t, :], rhs=kqT[s][:, PACK + j, :], start=True, stop=True
+                )
+            if j == 0:
+                p_bf[s] = work.tile([P, PACK, P, PACK], BF16, name="p_bf", align_bytes=64)
+            nc.scalar.activation(out=p_bf[s][:, j, :, :], in_=scores[:].rearrange("i t r -> i r t"), func=RELU)
+
+        def quantise_p(s):
+            p_words[s] = mx_operands.tile([P, CHUNK], U32, name="p_words", align_bytes=64)
+            p_scales[s] = mx_operands.tile([P, CHUNK], U8, name="p_scales", align_bytes=64)
+            nc.vector.quantize_mx(
+                out=p_words[s][:].bitcast(FP8X4),
+                scales=p_scales[s][:],
+                in_=p_bf[s][:].rearrange("i j r t -> i (j r t)"),
+            )
+
+        def regroup_v(s):
+            g, h = divmod(s, LOAD_SLICES)
+            v_bf[s] = work.tile([P, HEAD, PACK], BF16, name="v_bf", align_bytes=64)
+            nc.vector.tensor_copy(
+                out=v_bf[s][:].rearrange("i (c e) t -> i c t e", e=4),
+                in_=v_in[g][:, h].rearrange("i t (c e) -> i c t e", e=4),
+            )
+
+        def quantise_v(s):
+            v_words[s] = mx_operands.tile([P, HEAD], U32, name="v_words", align_bytes=64)
+            v_scales[s] = mx_operands.tile([P, HEAD], U8, name="v_scales", align_bytes=64)
+            nc.vector.quantize_mx(
+                out=v_words[s][:].bitcast(FP8X4),
+                scales=v_scales[s][:],
+                in_=v_bf[s][:].rearrange("i c t -> i (c t)"),
+            )
+
+        def p_times_v(s):
+            out_bank[s] = out_banks.tile([P, PACK, HEAD], F32, name="out_bank")
+            for j in range(PACK):
+                queries = slice(j * P, (j + 1) * P)
+                nc.tensor.matmul_mx(
+                    out=out_bank[s][:, j, :],
+                    lhsT=p_words[s][:, queries].bitcast(FP8X4),
+                    lhsT_scale=p_scales[s][:, queries],
+                    rhs=v_words[s][:].bitcast(FP8X4),
+                    rhs_scale=v_scales[s][:],
+                    start=True,
+                    stop=True,
+                )
+
+        def copy_and_store_out(s):
+            out_sb[s] = results.tile([P, PACK, HEAD], F32, name="out_sb")
+            nc.vector.tensor_copy(out=out_sb[s][:], in_=out_bank[s][:])
+            nc.sync.dma_start(out=out_rows[:, s], in_=out_sb[s][:])
+
+        def when_valid(stage, s):
+            if 0 <= s < SLICES:
+                stage(s)
+
+        for i in range(-1, SLICES + 3):
+            when_valid(quantise_p, i - 2)
+            when_valid(quantise_v, i - 1)
+            if 0 <= i < SLICES:
+                scores_and_relu(i, 0)
+            when_valid(transpose_k_and_q, i + 1)
+            if 0 <= i < SLICES:
+                scores_and_relu(i, 1)
+            when_valid(p_times_v, i - 2)
+            if 0 <= i < SLICES:
+                scores_and_relu(i, 2)
+                scores_and_relu(i, 3)
+            when_valid(copy_and_store_out, i - 3)
+            when_valid(regroup_v, i)
+            when_valid(copy_kT_and_qT, i + 1)

@@ -16,6 +16,7 @@ SLICES = 32
 CHUNK = 512
 HEAD = 128
 LOAD_SLICES = 2
+VECTOR_RELU_EVERY = 4
 
 FLOPS = 2 * 2 * SLICES * CHUNK * CHUNK * HEAD
 
@@ -32,6 +33,7 @@ def tile_normlocalattention_pa_kernel(tc, q_chunks, k_chunks, v_chunks, out):
         const = ctx.enter_context(tc.tile_pool(name="const", bufs=1))
         inputs = ctx.enter_context(tc.tile_pool(name="inputs", bufs=1))
         work = ctx.enter_context(tc.tile_pool(name="work", bufs=2))
+        v_stage = ctx.enter_context(tc.tile_pool(name="v_stage", bufs=1))
         mx_operands = ctx.enter_context(tc.tile_pool(name="mx_operands", bufs=3))
         results = ctx.enter_context(tc.tile_pool(name="results", bufs=SLICES))
         transposed_banks = ctx.enter_context(tc.psum_pool(name="transposed_banks", bufs=2))
@@ -72,7 +74,11 @@ def tile_normlocalattention_pa_kernel(tc, q_chunks, k_chunks, v_chunks, out):
                 )
             if j == 0:
                 p_bf[s] = work.tile([P, PACK, P, PACK], BF16, name="p_bf", align_bytes=64)
-            nc.scalar.activation(out=p_bf[s][:, j, :, :], in_=scores[:].rearrange("i t r -> i r t"), func=RELU)
+            words_first = scores[:].rearrange("i t r -> i r t")
+            if j == 0 and s % VECTOR_RELU_EVERY == 0:
+                nc.vector.tensor_scalar_max(out=p_bf[s][:, j, :, :], in0=words_first, scalar1=0.0)
+            else:
+                nc.scalar.activation(out=p_bf[s][:, j, :, :], in_=words_first, func=RELU)
 
         def quantise_p(s):
             p_words[s] = mx_operands.tile([P, CHUNK], U32, name="p_words", align_bytes=64)
@@ -85,10 +91,14 @@ def tile_normlocalattention_pa_kernel(tc, q_chunks, k_chunks, v_chunks, out):
 
         def regroup_v(s):
             g, h = divmod(s, LOAD_SLICES)
-            v_bf[s] = work.tile([P, HEAD, PACK], BF16, name="v_bf", align_bytes=64)
-            nc.vector.tensor_copy(
-                out=v_bf[s][:].rearrange("i (c e) t -> i c t e", e=4),
-                in_=v_in[g][:, h].rearrange("i t (c e) -> i c t e", e=4),
+            v_bf[s] = v_stage.tile([P, HEAD, PACK], BF16, name="v_bf", align_bytes=64)
+            nc.gpsimd.tensor_scalar(
+                out=v_bf[s][:],
+                in0=v_in[g][:, h].rearrange("i t c -> i c t"),
+                scalar1=1.0,
+                scalar2=0.0,
+                op0=mybir.AluOpType.mult,
+                op1=mybir.AluOpType.add,
             )
 
         def quantise_v(s):

@@ -15,8 +15,7 @@ PACK = 4
 SLICES = 32
 CHUNK = 512
 HEAD = 128
-LOAD_SLICES = 2
-VECTOR_RELU_EVERY = 4
+VECTOR_RELU_EVERY = 3
 
 FLOPS = 2 * 2 * SLICES * CHUNK * CHUNK * HEAD
 
@@ -41,11 +40,10 @@ def tile_normlocalattention_pa_kernel(tc, q_chunks, k_chunks, v_chunks, out):
         out_banks = ctx.enter_context(tc.psum_pool(name="out_banks", bufs=2))
 
         k_in, q_in, v_in = [], [], []
-        for g in range(SLICES // LOAD_SLICES):
-            slices = slice(g * LOAD_SLICES, (g + 1) * LOAD_SLICES)
+        for s in range(SLICES):
             for label, rows, tiles in (("k", k_rows, k_in), ("q", q_rows, q_in), ("v", v_rows, v_in)):
-                loaded = inputs.tile([P, LOAD_SLICES, PACK, HEAD], BF16, name="%s_in%d" % (label, g))
-                nc.sync.dma_start(out=loaded[:], in_=rows[:, slices])
+                loaded = inputs.tile([P, PACK, HEAD], BF16, name="%s_in%d" % (label, s))
+                nc.sync.dma_start(out=loaded[:], in_=rows[:, s])
                 tiles.append(loaded)
 
         identity = const.tile([P, P], BF16)
@@ -55,12 +53,11 @@ def tile_normlocalattention_pa_kernel(tc, q_chunks, k_chunks, v_chunks, out):
         v_bf, v_words, v_scales, out_bank, out_sb = {}, {}, {}, {}, {}
 
         def transpose_k_and_q(s):
-            g, h = divmod(s, LOAD_SLICES)
             kqT_bank[s] = transposed_banks.tile([P, 2 * PACK, P], BF16, name="kqT_bank")
             for t in range(PACK):
-                nc.tensor.transpose(kqT_bank[s][:, t, :], k_in[g][:, h, t, :], identity[:])
+                nc.tensor.transpose(kqT_bank[s][:, t, :], k_in[s][:, t, :], identity[:])
             for j in range(PACK):
-                nc.tensor.transpose(kqT_bank[s][:, PACK + j, :], q_in[g][:, h, j, :], identity[:])
+                nc.tensor.transpose(kqT_bank[s][:, PACK + j, :], q_in[s][:, j, :], identity[:])
 
         def copy_kT_and_qT(s):
             kqT[s] = work.tile([P, 2 * PACK, P], BF16, name="kqT")
@@ -75,7 +72,7 @@ def tile_normlocalattention_pa_kernel(tc, q_chunks, k_chunks, v_chunks, out):
             if j == 0:
                 p_bf[s] = work.tile([P, PACK, P, PACK], BF16, name="p_bf", align_bytes=64)
             words_first = scores[:].rearrange("i t r -> i r t")
-            if j == 0 and s % VECTOR_RELU_EVERY == 0:
+            if j == 0 and s % VECTOR_RELU_EVERY == 1:
                 nc.vector.tensor_scalar_max(out=p_bf[s][:, j, :, :], in0=words_first, scalar1=0.0)
             else:
                 nc.scalar.activation(out=p_bf[s][:, j, :, :], in_=words_first, func=RELU)
@@ -90,11 +87,10 @@ def tile_normlocalattention_pa_kernel(tc, q_chunks, k_chunks, v_chunks, out):
             )
 
         def regroup_v(s):
-            g, h = divmod(s, LOAD_SLICES)
             v_bf[s] = v_stage.tile([P, HEAD, PACK], BF16, name="v_bf", align_bytes=64)
             nc.gpsimd.tensor_scalar(
                 out=v_bf[s][:],
-                in0=v_in[g][:, h].rearrange("i t c -> i c t"),
+                in0=v_in[s][:].rearrange("i t c -> i c t"),
                 scalar1=1.0,
                 scalar2=0.0,
                 op0=mybir.AluOpType.mult,

@@ -15,7 +15,7 @@ PACK = 4
 SLICES = 32
 CHUNK = 512
 HEAD = 128
-VECTOR_RELU_EVERY = 3
+VECTOR_RELU_EVERY = 4
 
 FLOPS = 2 * 2 * SLICES * CHUNK * CHUNK * HEAD
 
@@ -72,7 +72,7 @@ def tile_normlocalattention_pa_kernel(tc, q_chunks, k_chunks, v_chunks, out):
             if j == 0:
                 p_bf[s] = work.tile([P, PACK, P, PACK], BF16, name="p_bf", align_bytes=64)
             words_first = scores[:].rearrange("i t r -> i r t")
-            if j == 0 and s % VECTOR_RELU_EVERY == 1:
+            if j == 0 and (SLICES - 1 - s) % VECTOR_RELU_EVERY == 0:
                 nc.vector.tensor_scalar_max(out=p_bf[s][:, j, :, :], in0=words_first, scalar1=0.0)
             else:
                 nc.scalar.activation(out=p_bf[s][:, j, :, :], in_=words_first, func=RELU)

@@ -16,6 +16,8 @@ SLICES = 32
 CHUNK = 512
 HEAD = 128
 VECTOR_RELU_EVERY = 4
+FIRST_SLICE_PARTS = ((0, PACK + 1), (PACK + 1, PACK - 1))
+LAST_SLICE_PARTS = ((0, 2), (2, 1), (3, 1))
 
 FLOPS = 2 * 2 * SLICES * CHUNK * CHUNK * HEAD
 
@@ -52,16 +54,16 @@ def tile_normlocalattention_pa_kernel(tc, q_chunks, k_chunks, v_chunks, out):
         kqT_bank, kqT, p_bf, p_words, p_scales = {}, {}, {}, {}, {}
         v_bf, v_words, v_scales, out_bank, out_sb = {}, {}, {}, {}, {}
 
-        def transpose_k_and_q(s):
-            kqT_bank[s] = transposed_banks.tile([P, 2 * PACK, P], BF16, name="kqT_bank")
-            for t in range(PACK):
-                nc.tensor.transpose(kqT_bank[s][:, t, :], k_in[s][:, t, :], identity[:])
-            for j in range(PACK):
-                nc.tensor.transpose(kqT_bank[s][:, PACK + j, :], q_in[s][:, j, :], identity[:])
+        def transpose_k_and_q(s, first=0, count=2 * PACK):
+            kqT_bank[s, first] = transposed_banks.tile([P, count, P], BF16, name="kqT_bank")
+            for block in range(first, first + count):
+                rows = k_in[s][:, block, :] if block < PACK else q_in[s][:, block - PACK, :]
+                nc.tensor.transpose(kqT_bank[s, first][:, block - first, :], rows, identity[:])
 
-        def copy_kT_and_qT(s):
-            kqT[s] = work.tile([P, 2 * PACK, P], BF16, name="kqT")
-            nc.vector.tensor_copy(out=kqT[s][:], in_=kqT_bank[s][:])
+        def copy_kT_and_qT(s, first=0, count=2 * PACK):
+            if first == 0:
+                kqT[s] = work.tile([P, 2 * PACK, P], BF16, name="kqT")
+            nc.vector.tensor_copy(out=kqT[s][:, first : first + count], in_=kqT_bank[s, first][:])
 
         def scores_and_relu(s, j):
             scores = score_banks.tile([P, PACK, P], F32, name="scores")
@@ -77,13 +79,15 @@ def tile_normlocalattention_pa_kernel(tc, q_chunks, k_chunks, v_chunks, out):
             else:
                 nc.scalar.activation(out=p_bf[s][:, j, :, :], in_=words_first, func=RELU)
 
-        def quantise_p(s):
-            p_words[s] = mx_operands.tile([P, CHUNK], U32, name="p_words", align_bytes=64)
-            p_scales[s] = mx_operands.tile([P, CHUNK], U8, name="p_scales", align_bytes=64)
+        def quantise_p(s, first=0, count=PACK):
+            if first == 0:
+                p_words[s] = mx_operands.tile([P, CHUNK], U32, name="p_words", align_bytes=64)
+                p_scales[s] = mx_operands.tile([P, CHUNK], U8, name="p_scales", align_bytes=64)
+            queries = slice(first * P, (first + count) * P)
             nc.vector.quantize_mx(
-                out=p_words[s][:].bitcast(FP8X4),
-                scales=p_scales[s][:],
-                in_=p_bf[s][:].rearrange("i j r t -> i (j r t)"),
+                out=p_words[s][:, queries].bitcast(FP8X4),
+                scales=p_scales[s][:, queries],
+                in_=p_bf[s][:, first : first + count].rearrange("i j r t -> i (j r t)"),
             )
 
         def regroup_v(s):
@@ -106,12 +110,12 @@ def tile_normlocalattention_pa_kernel(tc, q_chunks, k_chunks, v_chunks, out):
                 in_=v_bf[s][:].rearrange("i c t -> i (c t)"),
             )
 
-        def p_times_v(s):
-            out_bank[s] = out_banks.tile([P, PACK, HEAD], F32, name="out_bank")
-            for j in range(PACK):
-                queries = slice(j * P, (j + 1) * P)
+        def p_times_v(s, first=0, count=PACK, banks=out_banks, tag="out_bank"):
+            out_bank[s, first] = banks.tile([P, count, HEAD], F32, name=tag)
+            for j in range(count):
+                queries = slice((first + j) * P, (first + j + 1) * P)
                 nc.tensor.matmul_mx(
-                    out=out_bank[s][:, j, :],
+                    out=out_bank[s, first][:, j, :],
                     lhsT=p_words[s][:, queries].bitcast(FP8X4),
                     lhsT_scale=p_scales[s][:, queries],
                     rhs=v_words[s][:].bitcast(FP8X4),
@@ -120,27 +124,45 @@ def tile_normlocalattention_pa_kernel(tc, q_chunks, k_chunks, v_chunks, out):
                     stop=True,
                 )
 
-        def copy_and_store_out(s):
-            out_sb[s] = results.tile([P, PACK, HEAD], F32, name="out_sb")
-            nc.vector.tensor_copy(out=out_sb[s][:], in_=out_bank[s][:])
-            nc.sync.dma_start(out=out_rows[:, s], in_=out_sb[s][:])
+        def copy_and_store_out(s, first=0, count=PACK, on_scalar=False):
+            out_sb[s, first] = results.tile([P, count, HEAD], F32, name="out_sb")
+            if on_scalar:
+                nc.scalar.copy(out=out_sb[s, first][:], in_=out_bank[s, first][:])
+            else:
+                nc.vector.tensor_copy(out=out_sb[s, first][:], in_=out_bank[s, first][:])
+            nc.sync.dma_start(out=out_rows[:, s, first : first + count], in_=out_sb[s, first][:])
 
         def when_valid(stage, s):
             if 0 <= s < SLICES:
                 stage(s)
 
-        for i in range(-1, SLICES + 3):
+        LAST = SLICES - 1
+
+        for first, count in FIRST_SLICE_PARTS:
+            transpose_k_and_q(0, first, count)
+        for first, count in FIRST_SLICE_PARTS:
+            copy_kT_and_qT(0, first, count)
+
+        for i in range(SLICES):
             when_valid(quantise_p, i - 2)
             when_valid(quantise_v, i - 1)
-            if 0 <= i < SLICES:
-                scores_and_relu(i, 0)
+            scores_and_relu(i, 0)
             when_valid(transpose_k_and_q, i + 1)
-            if 0 <= i < SLICES:
-                scores_and_relu(i, 1)
+            scores_and_relu(i, 1)
             when_valid(p_times_v, i - 2)
-            if 0 <= i < SLICES:
-                scores_and_relu(i, 2)
-                scores_and_relu(i, 3)
+            scores_and_relu(i, 2)
+            scores_and_relu(i, 3)
             when_valid(copy_and_store_out, i - 3)
-            when_valid(regroup_v, i)
+            regroup_v(i)
             when_valid(copy_kT_and_qT, i + 1)
+
+        quantise_p(LAST - 1)
+        quantise_v(LAST)
+        p_times_v(LAST - 1)
+        copy_and_store_out(LAST - 2)
+        for first, count in LAST_SLICE_PARTS:
+            quantise_p(LAST, first, count)
+            p_times_v(LAST, first, count, score_banks, "scores")
+        copy_and_store_out(LAST - 1, on_scalar=True)
+        for first, count in LAST_SLICE_PARTS:
+            copy_and_store_out(LAST, first, count)

@@ -16,6 +16,7 @@ SLICES = 32
 CHUNK = 512
 HEAD = 128
 VECTOR_RELU_EVERY = 4
+WARM_UP_MATMULS = 10
 FIRST_SLICE_PARTS = ((0, PACK + 1), (PACK + 1, PACK - 1))
 LAST_SLICE_PARTS = ((0, 2), (2, 1), (3, 1))
 
@@ -50,6 +51,10 @@ def tile_normlocalattention_pa_kernel(tc, q_chunks, k_chunks, v_chunks, out):
 
         identity = const.tile([P, P], BF16)
         make_identity(nc, identity[:])
+
+        warm_bank = score_banks.tile([P, P], F32, name="scores")
+        for n in range(WARM_UP_MATMULS):
+            nc.tensor.matmul(warm_bank[:], lhsT=identity[:], rhs=identity[:], start=True, stop=True)
 
         kqT_bank, kqT, p_bf, p_words, p_scales = {}, {}, {}, {}, {}
         v_bf, v_words, v_scales, out_bank, out_sb = {}, {}, {}, {}, {}

@@ -34,7 +34,7 @@ def tile_normlocalattention_pa_kernel(tc, q_chunks, k_chunks, v_chunks, out):
         ctx.enter_context(tc.manual_schedule())
         const = ctx.enter_context(tc.tile_pool(name="const", bufs=1))
         inputs = ctx.enter_context(tc.tile_pool(name="inputs", bufs=1))
-        work = ctx.enter_context(tc.tile_pool(name="work", bufs=2))
+        work = ctx.enter_context(tc.tile_pool(name="work", bufs=3))
         v_stage = ctx.enter_context(tc.tile_pool(name="v_stage", bufs=1))
         mx_operands = ctx.enter_context(tc.tile_pool(name="mx_operands", bufs=3))
         results = ctx.enter_context(tc.tile_pool(name="results", bufs=SLICES))
@@ -155,11 +155,11 @@ def tile_normlocalattention_pa_kernel(tc, q_chunks, k_chunks, v_chunks, out):
             when_valid(transpose_k_and_q, i + 1)
             scores_and_relu(i, 1)
             when_valid(p_times_v, i - 2)
+            when_valid(copy_kT_and_qT, i + 1)
             scores_and_relu(i, 2)
             scores_and_relu(i, 3)
             when_valid(copy_and_store_out, i - 3)
             regroup_v(i)
-            when_valid(copy_kT_and_qT, i + 1)
 
         quantise_p(LAST - 1)
         quantise_v(LAST)

@@ -15,7 +15,7 @@ PACK = 4
 SLICES = 32
 CHUNK = 512
 HEAD = 128
-VECTOR_RELU_EVERY = 4
+VECTOR_SECOND_RELU_EVERY = 5
 WARM_UP_MATMULS = 10
 FIRST_SLICE_PARTS = ((0, PACK + 1), (PACK + 1, PACK - 1))
 LAST_SLICE_PARTS = ((0, 2), (2, 1), (3, 1))
@@ -57,7 +57,7 @@ def tile_normlocalattention_pa_kernel(tc, q_chunks, k_chunks, v_chunks, out):
             nc.tensor.matmul(warm_bank[:], lhsT=identity[:], rhs=identity[:], start=True, stop=True)
 
         kqT_bank, kqT, p_bf, p_words, p_scales = {}, {}, {}, {}, {}
-        v_bf, v_words, v_scales, out_bank, out_sb = {}, {}, {}, {}, {}
+        v_bf, v_words, v_scales, out_bank, out_sb, score_bank = {}, {}, {}, {}, {}, {}
 
         def transpose_k_and_q(s, first=0, count=2 * PACK):
             kqT_bank[s, first] = transposed_banks.tile([P, count, P], BF16, name="kqT_bank")
@@ -70,16 +70,18 @@ def tile_normlocalattention_pa_kernel(tc, q_chunks, k_chunks, v_chunks, out):
                 kqT[s] = work.tile([P, 2 * PACK, P], BF16, name="kqT")
             nc.vector.tensor_copy(out=kqT[s][:, first : first + count], in_=kqT_bank[s, first][:])
 
-        def scores_and_relu(s, j):
-            scores = score_banks.tile([P, PACK, P], F32, name="scores")
+        def scores(s, j):
+            score_bank[s, j] = score_banks.tile([P, PACK, P], F32, name="scores")
             for t in range(PACK):
                 nc.tensor.matmul(
-                    scores[:, t, :], lhsT=kqT[s][:, t, :], rhs=kqT[s][:, PACK + j, :], start=True, stop=True
+                    score_bank[s, j][:, t, :], lhsT=kqT[s][:, t, :], rhs=kqT[s][:, PACK + j, :], start=True, stop=True
                 )
+
+        def relu(s, j):
             if j == 0:
                 p_bf[s] = work.tile([P, PACK, P, PACK], BF16, name="p_bf", align_bytes=64)
-            words_first = scores[:].rearrange("i t r -> i r t")
-            if j == 0 and (SLICES - 1 - s) % VECTOR_RELU_EVERY == 0:
+            words_first = score_bank[s, j][:].rearrange("i t r -> i r t")
+            if j == 0 or (j == 1 and s % VECTOR_SECOND_RELU_EVERY == 0):
                 nc.vector.tensor_scalar_max(out=p_bf[s][:, j, :, :], in0=words_first, scalar1=0.0)
             else:
                 nc.scalar.activation(out=p_bf[s][:, j, :, :], in_=words_first, func=RELU)
@@ -151,14 +153,19 @@ def tile_normlocalattention_pa_kernel(tc, q_chunks, k_chunks, v_chunks, out):
         for i in range(SLICES):
             when_valid(quantise_p, i - 2)
             when_valid(quantise_v, i - 1)
-            scores_and_relu(i, 0)
+            scores(i, 0)
+            relu(i, 0)
+            if i >= 3:
+                copy_and_store_out(i - 3, on_scalar=True)
             when_valid(transpose_k_and_q, i + 1)
-            scores_and_relu(i, 1)
+            scores(i, 1)
             when_valid(p_times_v, i - 2)
             when_valid(copy_kT_and_qT, i + 1)
-            scores_and_relu(i, 2)
-            scores_and_relu(i, 3)
-            when_valid(copy_and_store_out, i - 3)
+            relu(i, 1)
+            scores(i, 2)
+            relu(i, 2)
+            scores(i, 3)
+            relu(i, 3)
             regroup_v(i)
 
         quantise_p(LAST - 1)

@@ -15,7 +15,7 @@ PACK = 4
 SLICES = 32
 CHUNK = 512
 HEAD = 128
-VECTOR_SECOND_RELU_EVERY = 5
+VECTOR_SECOND_RELU_EVERY = 4
 WARM_UP_MATMULS = 10
 FIRST_SLICE_PARTS = ((0, PACK + 1), (PACK + 1, PACK - 1))
 LAST_SLICE_PARTS = ((0, 2), (2, 1), (3, 1))
@@ -81,7 +81,7 @@ def tile_normlocalattention_pa_kernel(tc, q_chunks, k_chunks, v_chunks, out):
             if j == 0:
                 p_bf[s] = work.tile([P, PACK, P, PACK], BF16, name="p_bf", align_bytes=64)
             words_first = score_bank[s, j][:].rearrange("i t r -> i r t")
-            if j == 0 or (j == 1 and s % VECTOR_SECOND_RELU_EVERY == 0):
+            if (j == 0 and s > 0) or (j == 1 and s % VECTOR_SECOND_RELU_EVERY == 1):
                 nc.vector.tensor_scalar_max(out=p_bf[s][:, j, :, :], in0=words_first, scalar1=0.0)
             else:
                 nc.scalar.activation(out=p_bf[s][:, j, :, :], in_=words_first, func=RELU)

from contextlib import ExitStack

import concourse.mybir as mybir
from concourse.masks import make_identity

BF16 = mybir.dt.bfloat16
F32 = mybir.dt.float32
U32 = mybir.dt.uint32
U8 = mybir.dt.uint8
FP8X4 = mybir.dt.float8_e4m3fn_x4
RELU = mybir.ActivationFunctionType.Relu

P = 128
PACK = 4
SLICES = 32
CHUNK = 512
HEAD = 128
VECTOR_SECOND_RELU_EVERY = 4
WARM_UP_MATMULS = 10
FIRST_SLICE_PARTS = ((0, PACK + 1), (PACK + 1, PACK - 1))
LAST_SLICE_PARTS = ((0, 2), (2, 1), (3, 1))

FLOPS = 2 * 2 * SLICES * CHUNK * CHUNK * HEAD


def tile_normlocalattention_pa_kernel(tc, q_chunks, k_chunks, v_chunks, out):
    nc = tc.nc
    q_rows = q_chunks.rearrange("n g (i j) d -> i (n g) j d", j=PACK)
    k_rows = k_chunks.rearrange("n g (i j) d -> i (n g) j d", j=PACK)
    v_rows = v_chunks.rearrange("n g (i j) d -> i (n g) j d", j=PACK)
    out_rows = out.rearrange("n g (i j) d -> i (n g) j d", j=PACK)

    with ExitStack() as ctx:
        ctx.enter_context(tc.manual_schedule())
        const = ctx.enter_context(tc.tile_pool(name="const", bufs=1))
        inputs = ctx.enter_context(tc.tile_pool(name="inputs", bufs=1))
        work = ctx.enter_context(tc.tile_pool(name="work", bufs=3))
        v_stage = ctx.enter_context(tc.tile_pool(name="v_stage", bufs=1))
        mx_operands = ctx.enter_context(tc.tile_pool(name="mx_operands", bufs=3))
        results = ctx.enter_context(tc.tile_pool(name="results", bufs=SLICES))
        transposed_banks = ctx.enter_context(tc.psum_pool(name="transposed_banks", bufs=2))
        score_banks = ctx.enter_context(tc.psum_pool(name="score_banks", bufs=4))
        out_banks = ctx.enter_context(tc.psum_pool(name="out_banks", bufs=2))

        k_in, q_in, v_in = [], [], []
        for s in range(SLICES):
            for label, rows, tiles in (("k", k_rows, k_in), ("q", q_rows, q_in), ("v", v_rows, v_in)):
                loaded = inputs.tile([P, PACK, HEAD], BF16, name="%s_in%d" % (label, s))
                nc.sync.dma_start(out=loaded[:], in_=rows[:, s])
                tiles.append(loaded)

        identity = const.tile([P, P], BF16)
        make_identity(nc, identity[:])

        warm_bank = score_banks.tile([P, P], F32, name="scores")
        for n in range(WARM_UP_MATMULS):
            nc.tensor.matmul(warm_bank[:], lhsT=identity[:], rhs=identity[:], start=True, stop=True)

        kqT_bank, kqT, p_bf, p_words, p_scales = {}, {}, {}, {}, {}
        v_bf, v_words, v_scales, out_bank, out_sb, score_bank = {}, {}, {}, {}, {}, {}

        def transpose_k_and_q(s, first=0, count=2 * PACK):
            kqT_bank[s, first] = transposed_banks.tile([P, count, P], BF16, name="kqT_bank")
            for block in range(first, first + count):
                rows = k_in[s][:, block, :] if block < PACK else q_in[s][:, block - PACK, :]
                nc.tensor.transpose(kqT_bank[s, first][:, block - first, :], rows, identity[:])

        def copy_kT_and_qT(s, first=0, count=2 * PACK):
            if first == 0:
                kqT[s] = work.tile([P, 2 * PACK, P], BF16, name="kqT")
            nc.vector.tensor_copy(out=kqT[s][:, first : first + count], in_=kqT_bank[s, first][:])

        def scores(s, j):
            score_bank[s, j] = score_banks.tile([P, PACK, P], F32, name="scores")
            for t in range(PACK):
                nc.tensor.matmul(
                    score_bank[s, j][:, t, :], lhsT=kqT[s][:, t, :], rhs=kqT[s][:, PACK + j, :], start=True, stop=True
                )

        def relu(s, j):
            if j == 0:
                p_bf[s] = work.tile([P, PACK, P, PACK], BF16, name="p_bf", align_bytes=64)
            words_first = score_bank[s, j][:].rearrange("i t r -> i r t")
            if (j == 0 and s > 0) or (j == 1 and s % VECTOR_SECOND_RELU_EVERY == 1):
                nc.vector.tensor_scalar_max(out=p_bf[s][:, j, :, :], in0=words_first, scalar1=0.0)
            else:
                nc.scalar.activation(out=p_bf[s][:, j, :, :], in_=words_first, func=RELU)

        def quantise_p(s, first=0, count=PACK):
            if first == 0:
                p_words[s] = mx_operands.tile([P, CHUNK], U32, name="p_words", align_bytes=64)
                p_scales[s] = mx_operands.tile([P, CHUNK], U8, name="p_scales", align_bytes=64)
            queries = slice(first * P, (first + count) * P)
            nc.vector.quantize_mx(
                out=p_words[s][:, queries].bitcast(FP8X4),
                scales=p_scales[s][:, queries],
                in_=p_bf[s][:, first : first + count].rearrange("i j r t -> i (j r t)"),
            )

        def regroup_v(s):
            v_bf[s] = v_stage.tile([P, HEAD, PACK], BF16, name="v_bf", align_bytes=64)
            nc.gpsimd.tensor_scalar(
                out=v_bf[s][:],
                in0=v_in[s][:].rearrange("i t c -> i c t"),
                scalar1=1.0,
                scalar2=0.0,
                op0=mybir.AluOpType.mult,
                op1=mybir.AluOpType.add,
            )

        def quantise_v(s):
            v_words[s] = mx_operands.tile([P, HEAD], U32, name="v_words", align_bytes=64)
            v_scales[s] = mx_operands.tile([P, HEAD], U8, name="v_scales", align_bytes=64)
            nc.vector.quantize_mx(
                out=v_words[s][:].bitcast(FP8X4),
                scales=v_scales[s][:],
                in_=v_bf[s][:].rearrange("i c t -> i (c t)"),
            )

        def p_times_v(s, first=0, count=PACK, banks=out_banks, tag="out_bank"):
            out_bank[s, first] = banks.tile([P, count, HEAD], F32, name=tag)
            for j in range(count):
                queries = slice((first + j) * P, (first + j + 1) * P)
                nc.tensor.matmul_mx(
                    out=out_bank[s, first][:, j, :],
                    lhsT=p_words[s][:, queries].bitcast(FP8X4),
                    lhsT_scale=p_scales[s][:, queries],
                    rhs=v_words[s][:].bitcast(FP8X4),
                    rhs_scale=v_scales[s][:],
                    start=True,
                    stop=True,
                )

        def copy_and_store_out(s, first=0, count=PACK, on_scalar=False):
            out_sb[s, first] = results.tile([P, count, HEAD], F32, name="out_sb")
            if on_scalar:
                nc.scalar.copy(out=out_sb[s, first][:], in_=out_bank[s, first][:])
            else:
                nc.vector.tensor_copy(out=out_sb[s, first][:], in_=out_bank[s, first][:])
            nc.sync.dma_start(out=out_rows[:, s, first : first + count], in_=out_sb[s, first][:])

        def when_valid(stage, s):
            if 0 <= s < SLICES:
                stage(s)

        LAST = SLICES - 1

        for first, count in FIRST_SLICE_PARTS:
            transpose_k_and_q(0, first, count)
        for first, count in FIRST_SLICE_PARTS:
            copy_kT_and_qT(0, first, count)

        for i in range(SLICES):
            when_valid(quantise_p, i - 2)
            when_valid(quantise_v, i - 1)
            scores(i, 0)
            relu(i, 0)
            if i >= 3:
                copy_and_store_out(i - 3, on_scalar=True)
            when_valid(transpose_k_and_q, i + 1)
            scores(i, 1)
            when_valid(p_times_v, i - 2)
            when_valid(copy_kT_and_qT, i + 1)
            relu(i, 1)
            scores(i, 2)
            relu(i, 2)
            scores(i, 3)
            relu(i, 3)
            regroup_v(i)

        quantise_p(LAST - 1)
        quantise_v(LAST)
        p_times_v(LAST - 1)
        copy_and_store_out(LAST - 2)
        for first, count in LAST_SLICE_PARTS:
            quantise_p(LAST, first, count)
            p_times_v(LAST, first, count, score_banks, "scores")
        copy_and_store_out(LAST - 1, on_scalar=True)
        for first, count in LAST_SLICE_PARTS:
            copy_and_store_out(LAST, first, count)
